import numpy as np
import ml_dtypes


def mxq(x, axis, fmt="e4m3"):
    dtype, down = {"e4m3": (ml_dtypes.float8_e4m3fn, 7), "e5m2": (ml_dtypes.float8_e5m2, 14)}[fmt]
    v = np.moveaxis(np.asarray(x, np.float32).astype(ml_dtypes.bfloat16).astype(np.float64), axis, -1)
    blocks = v.reshape(v.shape[:-1] + (-1, 32))
    amax = np.abs(blocks).max(-1, keepdims=True)
    byte = np.maximum(np.where(amax > 0, np.frexp(amax)[1] - 1 + 127, 0) - down, 1)
    scale = np.exp2(byte - 127.0)
    codes = (blocks / scale).astype(np.float32).astype(dtype).astype(np.float64)
    return np.moveaxis((codes * scale).reshape(v.shape), -1, axis)


WIDE = False


def mx_kscale(k):
    if not WIDE:
        return np.ones(k)
    levels = np.array([10, -10, 5, -5, 0])
    a = np.random.permutation(np.resize(levels, k // 512 * 4)).reshape(k // 512, 4)
    idx = np.arange(k)
    return np.exp2(a[idx // 512, idx % 128 // 32])


BF16 = ml_dtypes.bfloat16


def bf(x):
    return np.asarray(x, np.float32).astype(BF16)


def f64(x):
    return np.asarray(x).astype(np.float64)


N, E, HD, H1, H3, DM = 1024, 8192, 256, 1024, 128, 1024
C = 2 * HD


def setup_inputs():
    s = mx_kscale(N)
    t = mx_kscale(C)
    r = np.concatenate([np.full(HD, 2.0 / np.sqrt(HD)), np.full(HD, 8.0 / np.sqrt(N * HD))])
    return {
        "H_A": bf(np.random.standard_normal((N, E)) * 0.25 * s[:, None]),
        "H_mean_A": bf(np.random.standard_normal((N, HD)) * 0.35 / s[:, None] * t[HD:]),
        "H_mean_M": bf(np.random.standard_normal((E, HD)) * 0.35 * t[:HD]),
        "wEA1": bf(np.random.standard_normal((C, H3)) * (r / t)[:, None]),
        "bEA1": bf(np.random.standard_normal(H3) * 0.1),
    }


def reference(H_A, H_mean_A, H_mean_M, wEA1, bEA1):
    sum_A = mxq(f64(H_A), 0, "e4m3").T @ mxq(f64(H_mean_A), 0, "e4m3")
    EventA = np.concatenate([f64(H_mean_M), sum_A], axis=1)
    return np.maximum((mxq(EventA, 1, "e4m3") @ mxq(f64(wEA1), 0, "e4m3")) + f64(bEA1), 0.0)

@@ -1,0 +1,216 @@
+from contextlib import ExitStack
+
+import concourse.mybir as mybir
+from concourse.masks import make_identity
+
+FLOPS = 2 * 1024 * 8192 * 256 + 2 * 8192 * 512 * 128
+
+BF16 = mybir.dt.bfloat16
+F32 = mybir.dt.float32
+U32 = mybir.dt.uint32
+U8 = mybir.dt.uint8
+FP8X4 = mybir.dt.float8_e4m3fn_x4
+
+P = 128
+NODES = 1024
+EVENTS = 8192
+HD = 256
+H3 = 128
+GROUP = 512
+TILES = 4
+NG = EVENTS // GROUP
+CHUNKS = [1, 1, 2, 2, 2, 2, 2, 2, 1, 1]
+HM_PARTS = [2, 2, 4, 4, 4]
+RAW_BUFS = 5
+ODD_PLANE = (2, 0, 0)
+SCALAR_UNITS = [(g, 1) for g in range(0, NG, 2)]
+
+
+def tile_mymodel_icdm_pa_t_kernel(tc, H_A, H_mean_A, H_mean_M, wEA1, bEA1, out):
+    nc = tc.nc
+    with ExitStack() as ctx:
+        const = ctx.enter_context(tc.tile_pool(name="const", bufs=1))
+        rawp = ctx.enter_context(tc.tile_pool(name="rawp", bufs=RAW_BUFS))
+        work = ctx.enter_context(tc.tile_pool(name="work", bufs=3))
+        outp = ctx.enter_context(tc.tile_pool(name="outp", bufs=4))
+        ps1p = ctx.enter_context(tc.psum_pool(name="ps1p", bufs=6))
+        ps3p = ctx.enter_context(tc.psum_pool(name="ps3p", bufs=2))
+
+        ident = const.tile([P, P], BF16, name="ident")
+        make_identity(nc, ident[:])
+        ident32 = const.tile([P, P], F32, name="ident32")
+        make_identity(nc, ident32[:])
+        hm32 = const.tile([P, P], F32, name="hm32")
+
+        haraw = const.tile([P, 2, 4, HD], BF16, name="haraw")
+        bb16 = const.tile([P, H3], BF16, name="bb16")
+        nc.scalar.dma_start(out=bb16[:], in_=bEA1.partition_broadcast(P))
+
+        raws = {}
+        hm = const.tile([P, NG, TILES, HD], BF16, name="hm")
+        hm_src = H_mean_M.rearrange("(g q i) f -> q g (i f)", q=P, i=TILES)
+        wraw = const.tile([P, 4, H3], BF16, name="wraw")
+
+        def load_chunk(k, g0, n):
+            width = n * GROUP
+            raw = rawp.tile([P, 2, 4, width], BF16, name="raw", tag="raw")
+            for c in range(2):
+                nc.sync.dma_start(
+                    out=raw[:, c, :, :],
+                    in_=H_A[512 * c : 512 * c + 512, g0 * GROUP : g0 * GROUP + width].rearrange(
+                        "(p j) w -> p j w", j=4
+                    ),
+                )
+            for d in range(n):
+                raws[g0 + d] = (raw, d * GROUP)
+
+        def load_hm(g0, n):
+            nc.sync.dma_start(
+                out=hm[:, g0 : g0 + n, :, :].rearrange("q g i f -> q g (i f)"),
+                in_=hm_src[:, g0 : g0 + n, :],
+            )
+
+        progress = {"chunk": 0, "group": 0, "part": 0, "hm_group": 0}
+
+        def load_next():
+            k = progress["chunk"]
+            if k >= len(CHUNKS):
+                return
+            load_chunk(k, progress["group"], CHUNKS[k])
+            if k == 0:
+                nc.sync.dma_start(
+                    out=haraw[:].rearrange("p c j h -> p c (j h)"),
+                    in_=H_mean_A.rearrange("(c p j) h -> p c (j h)", c=2, j=4),
+                )
+                nc.sync.dma_start(out=wraw[:], in_=wEA1.rearrange("(t p) n -> p t n", p=P))
+            progress["chunk"] = k + 1
+            progress["group"] += CHUNKS[k]
+            while progress["part"] < len(HM_PARTS) and progress["hm_group"] < progress["group"] + 1:
+                load_hm(progress["hm_group"], HM_PARTS[progress["part"]])
+                progress["hm_group"] += HM_PARTS[progress["part"]]
+                progress["part"] += 1
+
+        for k in range(RAW_BUFS):
+            load_next()
+
+        hagrp = const.tile([P, 2, HD, 4], BF16, name="hagrp", align_bytes=64)
+        nc.vector.tensor_copy(out=hagrp[:], in_=haraw[:].rearrange("p c j h -> p c h j"))
+        hac = const.tile([P, 2 * HD], U32, name="hac", align_bytes=64)
+        has = const.tile([P, 2 * HD], U8, name="has", align_bytes=64)
+        nc.vector.quantize_mx(
+            out=hac[:].bitcast(FP8X4), scales=has[:], in_=hagrp[:].rearrange("p c h j -> p (c h j)")
+        )
+        wgrp = const.tile([P, H3, 4], BF16, name="wgrp", align_bytes=64)
+        nc.vector.tensor_copy(out=wgrp[:], in_=wraw[:].rearrange("p t n -> p n t"))
+        wc = const.tile([P, H3], U32, name="wc", align_bytes=64)
+        ws = const.tile([P, H3], U8, name="ws", align_bytes=64)
+        nc.vector.quantize_mx(
+            out=wc[:].bitcast(FP8X4), scales=ws[:], in_=wgrp[:].rearrange("p n t -> p (n t)")
+        )
+        bias = const.tile([P, TILES, H3], F32, name="bias")
+        nc.vector.tensor_copy(out=bias[:], in_=bb16[:].unsqueeze(1).to_broadcast([P, TILES, H3]))
+
+        st = {}
+
+        def regroup(g):
+            raw, w0 = raws[g]
+            grp = work.tile([P, 2, TILES, P, 4], BF16, name="grp", tag="grp", align_bytes=64)
+            for c in range(2):
+                src = raw[:, c, :, w0 : w0 + GROUP].rearrange("p t (q i) -> p q t i", i=TILES)
+                dst = grp[:, c, :, :, :].rearrange("p i q t -> p q t i")
+                if (g, c) in SCALAR_UNITS:
+                    nc.scalar.copy(out=dst, in_=src)
+                else:
+                    nc.vector.tensor_copy(out=dst, in_=src)
+            st[("grp", g)] = grp
+            if g + 1 == NG or raws[g + 1][1] == 0:
+                load_next()
+
+        def quant1(g):
+            grp = st[("grp", g)]
+            codes = work.tile([P, 2 * GROUP], U32, name="codes1", tag="codes1", align_bytes=64)
+            plane = work.tile([P, 2 * GROUP], U8, name="plane1", tag="plane1", align_bytes=64)
+            nc.vector.quantize_mx(
+                out=codes[:].bitcast(FP8X4),
+                scales=plane[:],
+                in_=grp[:].rearrange("p c i q t -> p (c i q t)"),
+            )
+            st[("c1", g)] = (codes, plane)
+
+        def mm1_evac(g):
+            codes, plane = st[("c1", g)]
+            grp2 = work.tile([P, TILES, P, 4], BF16, name="grp2", tag="grp2", align_bytes=64)
+            for i in range(TILES):
+                ps = ps1p.tile([P, 4, P], F32, name="ps1", tag="ps1")
+                for t in range(2):
+                    if (g, i, t) == ODD_PLANE:
+                        nc.gpsimd.tensor_copy(out=hm32[:], in_=hm[:, g, i, P * t : P * t + P])
+                        nc.tensor.transpose(ps[:, t, :], hm32[:], ident32[:])
+                    else:
+                        nc.tensor.matmul(
+                            out=ps[:, t, :],
+                            lhsT=hm[:, g, i, P * t : P * t + P],
+                            rhs=ident[:],
+                            start=True,
+                            stop=True,
+                        )
+                for e in range(2):
+                    for c in range(2):
+                        cols = slice(c * GROUP + i * P, c * GROUP + i * P + P)
+                        hcols = slice(c * HD + e * P, c * HD + e * P + P)
+                        nc.tensor.matmul_mx(
+                            out=ps[:, 2 + e, :],
+                            lhsT=hac[:, hcols].bitcast(FP8X4),
+                            lhsT_scale=has[:, hcols],
+                            rhs=codes[:, cols].bitcast(FP8X4),
+                            rhs_scale=plane[:, cols],
+                            start=(c == 0),
+                            stop=(c == 1),
+                        )
+                nc.scalar.copy(out=grp2[:, i, :, :], in_=ps[:].rearrange("p t q -> p q t"))
+            st[("grp2", g)] = grp2
+
+        def quant2(g):
+            grp2 = st[("grp2", g)]
+            codes = work.tile([P, GROUP], U32, name="codes2", tag="codes2", align_bytes=64)
+            plane = work.tile([P, GROUP], U8, name="plane2", tag="plane2", align_bytes=64)
+            nc.vector.quantize_mx(
+                out=codes[:].bitcast(FP8X4),
+                scales=plane[:],
+                in_=grp2[:].rearrange("p i q t -> p (i q t)"),
+            )
+            st[("c2", g)] = (codes, plane)
+
+        def mm2_out(g):
+            codes, plane = st[("c2", g)]
+            ps = ps3p.tile([P, TILES, H3], F32, name="ps3", tag="ps3")
+            for i in range(TILES):
+                cols = slice(i * P, i * P + P)
+                nc.tensor.matmul_mx(
+                    out=ps[:, i, :],
+                    lhsT=codes[:, cols].bitcast(FP8X4),
+                    lhsT_scale=plane[:, cols],
+                    rhs=wc[:].bitcast(FP8X4),
+                    rhs_scale=ws[:],
+                    start=True,
+                    stop=True,
+                )
+            o32 = outp.tile([P, TILES, H3], F32, name="o32", tag="o32")
+            nc.vector.tensor_tensor(out=o32[:], in0=ps[:], in1=bias[:], op=mybir.AluOpType.add)
+            nc.scalar.activation(out=o32[:], in_=o32[:], func=mybir.ActivationFunctionType.Relu)
+            nc.sync.dma_start(
+                out=out[g * GROUP : (g + 1) * GROUP, :].rearrange("(q i) f -> q (i f)", i=TILES),
+                in_=o32[:].rearrange("p i f -> p (i f)"),
+            )
+
+        for s in range(NG + 3):
+            if s < NG:
+                regroup(s)
+            if 0 <= s - 2 < NG:
+                quant2(s - 2)
+            if 0 <= s - 3 < NG:
+                mm2_out(s - 3)
+            if s < NG:
+                quant1(s)
+            if 0 <= s - 1 < NG:
+                mm1_evac(s - 1)

@@ -118,10 +118,11 @@ def tile_mymodel_icdm_pa_t_kernel(tc, H_A, H_mean_A, H_mean_M, wEA1, bEA1, out):
             for c in range(2):
                 src = raw[:, c, :, w0 : w0 + GROUP].rearrange("p t (q i) -> p q t i", i=TILES)
                 dst = grp[:, c, :, :, :].rearrange("p i q t -> p q t i")
-                if (g, c) in SCALAR_UNITS:
-                    nc.scalar.copy(out=dst, in_=src)
-                else:
-                    nc.vector.tensor_copy(out=dst, in_=src)
+                for i0 in range(0, TILES, 2):
+                    if (g, c) in SCALAR_UNITS:
+                        nc.scalar.copy(out=dst[:, :, :, i0 : i0 + 2], in_=src[:, :, :, i0 : i0 + 2])
+                    else:
+                        nc.vector.tensor_copy(out=dst[:, :, :, i0 : i0 + 2], in_=src[:, :, :, i0 : i0 + 2])
             st[("grp", g)] = grp
             if g + 1 == NG or raws[g + 1][1] == 0:
                 load_next()

@@ -12,10 +12,9 @@ U8 = mybir.dt.uint8
 FP8X4 = mybir.dt.float8_e4m3fn_x4
 
 P = 128
-NODES = 1024
-EVENTS = 8192
 HD = 256
 H3 = 128
+EVENTS = 8192
 GROUP = 512
 TILES = 4
 NG = EVENTS // GROUP
@@ -23,7 +22,15 @@ CHUNKS = [1, 1, 2, 2, 2, 2, 2, 2, 1, 1]
 HM_PARTS = [2, 2, 4, 4, 4]
 RAW_BUFS = 5
 ODD_PLANE = (2, 0, 0)
-SCALAR_UNITS = [(g, 1) for g in range(0, NG, 2)]
+PINNED = True
+
+
+def scalar_units(g):
+    return [(1, 0), (1, 2)] if g < 2 else [(1, 2)]
+
+
+def vector_evacs(g):
+    return [2, 3] if g >= NG - 1 else []
 
 
 def tile_mymodel_icdm_pa_t_kernel(tc, H_A, H_mean_A, H_mean_M, wEA1, bEA1, out):
@@ -35,6 +42,8 @@ def tile_mymodel_icdm_pa_t_kernel(tc, H_A, H_mean_A, H_mean_M, wEA1, bEA1, out):
         outp = ctx.enter_context(tc.tile_pool(name="outp", bufs=4))
         ps1p = ctx.enter_context(tc.psum_pool(name="ps1p", bufs=6))
         ps3p = ctx.enter_context(tc.psum_pool(name="ps3p", bufs=2))
+        if PINNED:
+            ctx.enter_context(tc.manual_schedule())
 
         ident = const.tile([P, P], BF16, name="ident")
         make_identity(nc, ident[:])
@@ -51,7 +60,7 @@ def tile_mymodel_icdm_pa_t_kernel(tc, H_A, H_mean_A, H_mean_M, wEA1, bEA1, out):
         hm_src = H_mean_M.rearrange("(g q i) f -> q g (i f)", q=P, i=TILES)
         wraw = const.tile([P, 4, H3], BF16, name="wraw")
 
-        def load_chunk(k, g0, n):
+        def load_chunk(g0, n):
             width = n * GROUP
             raw = rawp.tile([P, 2, 4, width], BF16, name="raw", tag="raw")
             for c in range(2):
@@ -76,16 +85,17 @@ def tile_mymodel_icdm_pa_t_kernel(tc, H_A, H_mean_A, H_mean_M, wEA1, bEA1, out):
             k = progress["chunk"]
             if k >= len(CHUNKS):
                 return
-            load_chunk(k, progress["group"], CHUNKS[k])
+            load_chunk(progress["group"], CHUNKS[k])
             if k == 0:
                 nc.sync.dma_start(
                     out=haraw[:].rearrange("p c j h -> p c (j h)"),
                     in_=H_mean_A.rearrange("(c p j) h -> p c (j h)", c=2, j=4),
                 )
+            if k == 1:
                 nc.sync.dma_start(out=wraw[:], in_=wEA1.rearrange("(t p) n -> p t n", p=P))
             progress["chunk"] = k + 1
             progress["group"] += CHUNKS[k]
-            while progress["part"] < len(HM_PARTS) and progress["hm_group"] < progress["group"] + 1:
+            while progress["part"] < len(HM_PARTS) and progress["hm_group"] < progress["group"] - 1:
                 load_hm(progress["hm_group"], HM_PARTS[progress["part"]])
                 progress["hm_group"] += HM_PARTS[progress["part"]]
                 progress["part"] += 1
@@ -93,22 +103,31 @@ def tile_mymodel_icdm_pa_t_kernel(tc, H_A, H_mean_A, H_mean_M, wEA1, bEA1, out):
         for k in range(RAW_BUFS):
             load_next()
 
+        og, oi, ot = ODD_PLANE
+        nc.gpsimd.tensor_copy(out=hm32[:], in_=hm[:, og, oi, P * ot : P * ot + P])
+
         hagrp = const.tile([P, 2, HD, 4], BF16, name="hagrp", align_bytes=64)
-        nc.vector.tensor_copy(out=hagrp[:], in_=haraw[:].rearrange("p c j h -> p c h j"))
         hac = const.tile([P, 2 * HD], U32, name="hac", align_bytes=64)
         has = const.tile([P, 2 * HD], U8, name="has", align_bytes=64)
-        nc.vector.quantize_mx(
-            out=hac[:].bitcast(FP8X4), scales=has[:], in_=hagrp[:].rearrange("p c h j -> p (c h j)")
-        )
         wgrp = const.tile([P, H3, 4], BF16, name="wgrp", align_bytes=64)
-        nc.vector.tensor_copy(out=wgrp[:], in_=wraw[:].rearrange("p t n -> p n t"))
         wc = const.tile([P, H3], U32, name="wc", align_bytes=64)
         ws = const.tile([P, H3], U8, name="ws", align_bytes=64)
-        nc.vector.quantize_mx(
-            out=wc[:].bitcast(FP8X4), scales=ws[:], in_=wgrp[:].rearrange("p n t -> p (n t)")
-        )
         bias = const.tile([P, TILES, H3], F32, name="bias")
-        nc.vector.tensor_copy(out=bias[:], in_=bb16[:].unsqueeze(1).to_broadcast([P, TILES, H3]))
+
+        def prep_ha_copy():
+            nc.vector.tensor_copy(out=hagrp[:], in_=haraw[:].rearrange("p c j h -> p c h j"))
+
+        def prep_ha_quant():
+            nc.vector.quantize_mx(
+                out=hac[:].bitcast(FP8X4), scales=has[:], in_=hagrp[:].rearrange("p c h j -> p (c h j)")
+            )
+
+        def prep_w():
+            nc.vector.tensor_copy(out=wgrp[:], in_=wraw[:].rearrange("p t n -> p n t"))
+            nc.vector.tensor_copy(out=bias[:], in_=bb16[:].unsqueeze(1).to_broadcast([P, TILES, H3]))
+            nc.vector.quantize_mx(
+                out=wc[:].bitcast(FP8X4), scales=ws[:], in_=wgrp[:].rearrange("p n t -> p (n t)")
+            )
 
         st = {}
 
@@ -119,7 +138,7 @@ def tile_mymodel_icdm_pa_t_kernel(tc, H_A, H_mean_A, H_mean_M, wEA1, bEA1, out):
                 src = raw[:, c, :, w0 : w0 + GROUP].rearrange("p t (q i) -> p q t i", i=TILES)
                 dst = grp[:, c, :, :, :].rearrange("p i q t -> p q t i")
                 for i0 in range(0, TILES, 2):
-                    if (g, c) in SCALAR_UNITS:
+                    if (c, i0) in scalar_units(g):
                         nc.scalar.copy(out=dst[:, :, :, i0 : i0 + 2], in_=src[:, :, :, i0 : i0 + 2])
                     else:
                         nc.vector.tensor_copy(out=dst[:, :, :, i0 : i0 + 2], in_=src[:, :, :, i0 : i0 + 2])
@@ -138,14 +157,12 @@ def tile_mymodel_icdm_pa_t_kernel(tc, H_A, H_mean_A, H_mean_M, wEA1, bEA1, out):
             )
             st[("c1", g)] = (codes, plane)
 
-        def mm1_evac(g):
+        def mm1(g):
             codes, plane = st[("c1", g)]
-            grp2 = work.tile([P, TILES, P, 4], BF16, name="grp2", tag="grp2", align_bytes=64)
             for i in range(TILES):
                 ps = ps1p.tile([P, 4, P], F32, name="ps1", tag="ps1")
                 for t in range(2):
                     if (g, i, t) == ODD_PLANE:
-                        nc.gpsimd.tensor_copy(out=hm32[:], in_=hm[:, g, i, P * t : P * t + P])
                         nc.tensor.transpose(ps[:, t, :], hm32[:], ident32[:])
                     else:
                         nc.tensor.matmul(
@@ -168,7 +185,16 @@ def tile_mymodel_icdm_pa_t_kernel(tc, H_A, H_mean_A, H_mean_M, wEA1, bEA1, out):
                             start=(c == 0),
                             stop=(c == 1),
                         )
-                nc.scalar.copy(out=grp2[:, i, :, :], in_=ps[:].rearrange("p t q -> p q t"))
+                st[("ps1", g, i)] = ps
+
+        def evac(g):
+            grp2 = work.tile([P, TILES, P, 4], BF16, name="grp2", tag="grp2", align_bytes=64)
+            for i in range(TILES):
+                ps = st[("ps1", g, i)]
+                if i in vector_evacs(g):
+                    nc.vector.tensor_copy(out=grp2[:, i, :, :], in_=ps[:].rearrange("p t q -> p q t"))
+                else:
+                    nc.scalar.copy(out=grp2[:, i, :, :], in_=ps[:].rearrange("p t q -> p q t"))
             st[("grp2", g)] = grp2
 
         def quant2(g):
@@ -182,7 +208,7 @@ def tile_mymodel_icdm_pa_t_kernel(tc, H_A, H_mean_A, H_mean_M, wEA1, bEA1, out):
             )
             st[("c2", g)] = (codes, plane)
 
-        def mm2_out(g):
+        def mm2(g):
             codes, plane = st[("c2", g)]
             ps = ps3p.tile([P, TILES, H3], F32, name="ps3", tag="ps3")
             for i in range(TILES):
@@ -196,22 +222,45 @@ def tile_mymodel_icdm_pa_t_kernel(tc, H_A, H_mean_A, H_mean_M, wEA1, bEA1, out):
                     start=True,
                     stop=True,
                 )
+            st[("ps3", g)] = ps
+
+        def add_bias(g):
             o32 = outp.tile([P, TILES, H3], F32, name="o32", tag="o32")
-            nc.vector.tensor_tensor(out=o32[:], in0=ps[:], in1=bias[:], op=mybir.AluOpType.add)
+            nc.vector.tensor_tensor(out=o32[:], in0=st[("ps3", g)][:], in1=bias[:], op=mybir.AluOpType.add)
+            st[("o32", g)] = o32
+
+        def relu_store(g):
+            o32 = st[("o32", g)]
             nc.scalar.activation(out=o32[:], in_=o32[:], func=mybir.ActivationFunctionType.Relu)
             nc.sync.dma_start(
                 out=out[g * GROUP : (g + 1) * GROUP, :].rearrange("(q i) f -> q (i f)", i=TILES),
                 in_=o32[:].rearrange("p i f -> p (i f)"),
             )
 
-        for s in range(NG + 3):
-            if s < NG:
+        def live(g):
+            return 0 <= g < NG
+
+        for s in range(NG + 5):
+            if live(s):
                 regroup(s)
-            if 0 <= s - 2 < NG:
-                quant2(s - 2)
-            if 0 <= s - 3 < NG:
-                mm2_out(s - 3)
-            if s < NG:
-                quant1(s)
-            if 0 <= s - 1 < NG:
-                mm1_evac(s - 1)
+            if s == 0:
+                prep_ha_copy()
+            if s == 2:
+                prep_w()
+            if s >= NG and live(s - 1):
+                quant1(s - 1)
+            if live(s - 4):
+                add_bias(s - 4)
+            if live(s - 3):
+                quant2(s - 3)
+                mm2(s - 3)
+            if s == 1:
+                prep_ha_quant()
+            if s < NG and live(s - 1):
+                quant1(s - 1)
+            if live(s - 2):
+                evac(s - 2)
+            if live(s - 1):
+                mm1(s - 1)
+            if live(s - 4):
+                relu_store(s - 4)

@@ -18,15 +18,15 @@ EVENTS = 8192
 GROUP = 512
 TILES = 4
 NG = EVENTS // GROUP
-CHUNKS = [1, 1, 2, 2, 2, 2, 2, 2, 1, 1]
-HM_PARTS = [2, 2, 4, 4, 4]
-RAW_BUFS = 5
+CHUNKS = [1,1,1,1,2,2,2,2,2,1,1]
+HM_PARTS = [2,2,2,2,4,4]
+RAW_BUFS = 3
 ODD_PLANE = (2, 0, 0)
 PINNED = True
 
 
 def scalar_units(g):
-    return [(1, 0), (1, 2)] if g < 2 else [(1, 2)]
+    return [(1, 0), (1, 2)] if g in (0, 1, 5, 10) else [(1, 2)]
 
 
 def vector_evacs(g):
@@ -39,7 +39,7 @@ def tile_mymodel_icdm_pa_t_kernel(tc, H_A, H_mean_A, H_mean_M, wEA1, bEA1, out):
         const = ctx.enter_context(tc.tile_pool(name="const", bufs=1))
         rawp = ctx.enter_context(tc.tile_pool(name="rawp", bufs=RAW_BUFS))
         work = ctx.enter_context(tc.tile_pool(name="work", bufs=3))
-        outp = ctx.enter_context(tc.tile_pool(name="outp", bufs=4))
+        outp = ctx.enter_context(tc.tile_pool(name="outp", bufs=8))
         ps1p = ctx.enter_context(tc.psum_pool(name="ps1p", bufs=6))
         ps3p = ctx.enter_context(tc.psum_pool(name="ps3p", bufs=2))
         if PINNED:
@@ -103,9 +103,6 @@ def tile_mymodel_icdm_pa_t_kernel(tc, H_A, H_mean_A, H_mean_M, wEA1, bEA1, out):
         for k in range(RAW_BUFS):
             load_next()
 
-        og, oi, ot = ODD_PLANE
-        nc.gpsimd.tensor_copy(out=hm32[:], in_=hm[:, og, oi, P * ot : P * ot + P])
-
         hagrp = const.tile([P, 2, HD, 4], BF16, name="hagrp", align_bytes=64)
         hac = const.tile([P, 2 * HD], U32, name="hac", align_bytes=64)
         has = const.tile([P, 2 * HD], U8, name="has", align_bytes=64)
@@ -163,6 +160,7 @@ def tile_mymodel_icdm_pa_t_kernel(tc, H_A, H_mean_A, H_mean_M, wEA1, bEA1, out):
                 ps = ps1p.tile([P, 4, P], F32, name="ps1", tag="ps1")
                 for t in range(2):
                     if (g, i, t) == ODD_PLANE:
+                        nc.gpsimd.tensor_copy(out=hm32[:], in_=hm[:, g, i, P * t : P * t + P])
                         nc.tensor.transpose(ps[:, t, :], hm32[:], ident32[:])
                     else:
                         nc.tensor.matmul(
@@ -240,27 +238,24 @@ def tile_mymodel_icdm_pa_t_kernel(tc, H_A, H_mean_A, H_mean_M, wEA1, bEA1, out):
         def live(g):
             return 0 <= g < NG
 
-        for s in range(NG + 5):
+        for s in range(NG + 4):
             if live(s):
                 regroup(s)
             if s == 0:
                 prep_ha_copy()
-            if s == 2:
-                prep_w()
-            if s >= NG and live(s - 1):
-                quant1(s - 1)
-            if live(s - 4):
-                add_bias(s - 4)
-            if live(s - 3):
-                quant2(s - 3)
-                mm2(s - 3)
-            if s == 1:
                 prep_ha_quant()
-            if s < NG and live(s - 1):
-                quant1(s - 1)
+            if s == 1:
+                prep_w()
+            if live(s - 3):
+                add_bias(s - 3)
             if live(s - 2):
-                evac(s - 2)
+                quant2(s - 2)
+                mm2(s - 2)
+            if live(s):
+                quant1(s)
             if live(s - 1):
-                mm1(s - 1)
-            if live(s - 4):
-                relu_store(s - 4)
+                evac(s - 1)
+            if live(s):
+                mm1(s)
+            if live(s - 3):
+                relu_store(s - 3)

@@ -57,7 +57,7 @@ def tile_mymodel_icdm_pa_t_kernel(tc, H_A, H_mean_A, H_mean_M, wEA1, bEA1, out):
 
         raws = {}
         hm = const.tile([P, NG, TILES, HD], BF16, name="hm")
-        hm_src = H_mean_M.rearrange("(g q i) f -> q g (i f)", q=P, i=TILES)
+        hm_src = H_mean_M.rearrange("(x q) f -> q x f", q=P)
         wraw = const.tile([P, 4, H3], BF16, name="wraw")
 
         def load_chunk(g0, n):
@@ -75,8 +75,8 @@ def tile_mymodel_icdm_pa_t_kernel(tc, H_A, H_mean_A, H_mean_M, wEA1, bEA1, out):
 
         def load_hm(g0, n):
             nc.sync.dma_start(
-                out=hm[:, g0 : g0 + n, :, :].rearrange("q g i f -> q g (i f)"),
-                in_=hm_src[:, g0 : g0 + n, :],
+                out=hm[:, g0 : g0 + n, :, :].rearrange("q g i f -> q (g i) f"),
+                in_=hm_src[:, g0 * TILES : (g0 + n) * TILES, :],
             )
 
         progress = {"chunk": 0, "group": 0, "part": 0, "hm_group": 0}
@@ -132,13 +132,15 @@ def tile_mymodel_icdm_pa_t_kernel(tc, H_A, H_mean_A, H_mean_M, wEA1, bEA1, out):
             raw, w0 = raws[g]
             grp = work.tile([P, 2, TILES, P, 4], BF16, name="grp", tag="grp", align_bytes=64)
             for c in range(2):
-                src = raw[:, c, :, w0 : w0 + GROUP].rearrange("p t (q i) -> p q t i", i=TILES)
-                dst = grp[:, c, :, :, :].rearrange("p i q t -> p q t i")
                 for i0 in range(0, TILES, 2):
+                    src = raw[:, c, :, w0 + i0 * P : w0 + (i0 + 2) * P].rearrange("p t (b a) -> p b t a", a=4)
+                    dst = grp[:, c, i0 : i0 + 2, :, :].rearrange("p i q t -> p (i q) t").rearrange(
+                        "p (b a) t -> p b t a", a=4
+                    )
                     if (c, i0) in scalar_units(g):
-                        nc.scalar.copy(out=dst[:, :, :, i0 : i0 + 2], in_=src[:, :, :, i0 : i0 + 2])
+                        nc.scalar.copy(out=dst, in_=src)
                     else:
-                        nc.vector.tensor_copy(out=dst[:, :, :, i0 : i0 + 2], in_=src[:, :, :, i0 : i0 + 2])
+                        nc.vector.tensor_copy(out=dst, in_=src)
             st[("grp", g)] = grp
             if g + 1 == NG or raws[g + 1][1] == 0:
                 load_next()
@@ -231,8 +233,8 @@ def tile_mymodel_icdm_pa_t_kernel(tc, H_A, H_mean_A, H_mean_M, wEA1, bEA1, out):
             o32 = st[("o32", g)]
             nc.scalar.activation(out=o32[:], in_=o32[:], func=mybir.ActivationFunctionType.Relu)
             nc.sync.dma_start(
-                out=out[g * GROUP : (g + 1) * GROUP, :].rearrange("(q i) f -> q (i f)", i=TILES),
-                in_=o32[:].rearrange("p i f -> p (i f)"),
+                out=out[g * GROUP : (g + 1) * GROUP, :].rearrange("(i q) f -> q i f", i=TILES),
+                in_=o32[:],
             )
 
         def live(g):

@@ -22,7 +22,7 @@ CHUNKS = [1,1,1,1,2,2,2,2,2,1,1]
 HM_PARTS = [2,2,2,2,4,4]
 RAW_BUFS = 3
 ODD_PLANE = (2, 0, 0)
-PINNED = True
+PINNED = False
 
 
 def scalar_units(g):
@@ -132,12 +132,14 @@ def tile_mymodel_icdm_pa_t_kernel(tc, H_A, H_mean_A, H_mean_M, wEA1, bEA1, out):
             raw, w0 = raws[g]
             grp = work.tile([P, 2, TILES, P, 4], BF16, name="grp", tag="grp", align_bytes=64)
             for c in range(2):
-                for i0 in range(0, TILES, 2):
-                    src = raw[:, c, :, w0 + i0 * P : w0 + (i0 + 2) * P].rearrange("p t (b a) -> p b t a", a=4)
-                    dst = grp[:, c, i0 : i0 + 2, :, :].rearrange("p i q t -> p (i q) t").rearrange(
+                on_scalar = [i0 for i0 in range(0, TILES, 2) if (c, i0) in scalar_units(g)]
+                pieces = [(0, TILES)] if not on_scalar else [(0, 2), (2, 4)]
+                for i0, i1 in pieces:
+                    src = raw[:, c, :, w0 + i0 * P : w0 + i1 * P].rearrange("p t (b a) -> p b t a", a=4)
+                    dst = grp[:, c, i0:i1, :, :].rearrange("p i q t -> p (i q) t").rearrange(
                         "p (b a) t -> p b t a", a=4
                     )
-                    if (c, i0) in scalar_units(g):
+                    if i0 in on_scalar:
                         nc.scalar.copy(out=dst, in_=src)
                     else:
                         nc.vector.tensor_copy(out=dst, in_=src)

@@ -9,6 +9,7 @@ BF16 = mybir.dt.bfloat16
 F32 = mybir.dt.float32
 U32 = mybir.dt.uint32
 U8 = mybir.dt.uint8
+I32 = mybir.dt.int32
 FP8X4 = mybir.dt.float8_e4m3fn_x4
 
 P = 128
@@ -26,7 +27,7 @@ PINNED = False
 
 
 def scalar_units(g):
-    return [(1, 0), (1, 2)] if g in (0, 1, 5, 10) else [(1, 2)]
+    return [(1, 0), (1, 2)] if g < 2 else ([(1, 2)] if g % 3 == 0 else [])
 
 
 def vector_evacs(g):
@@ -40,8 +41,9 @@ def tile_mymodel_icdm_pa_t_kernel(tc, H_A, H_mean_A, H_mean_M, wEA1, bEA1, out):
         rawp = ctx.enter_context(tc.tile_pool(name="rawp", bufs=RAW_BUFS))
         work = ctx.enter_context(tc.tile_pool(name="work", bufs=3))
         outp = ctx.enter_context(tc.tile_pool(name="outp", bufs=8))
-        ps1p = ctx.enter_context(tc.psum_pool(name="ps1p", bufs=6))
+        ps1p = ctx.enter_context(tc.psum_pool(name="ps1p", bufs=4))
         ps3p = ctx.enter_context(tc.psum_pool(name="ps3p", bufs=2))
+        ps4p = ctx.enter_context(tc.psum_pool(name="ps4p", bufs=2))
         if PINNED:
             ctx.enter_context(tc.manual_schedule())
 
@@ -52,12 +54,13 @@ def tile_mymodel_icdm_pa_t_kernel(tc, H_A, H_mean_A, H_mean_M, wEA1, bEA1, out):
         hm32 = const.tile([P, P], F32, name="hm32")
 
         haraw = const.tile([P, 2, 4, HD], BF16, name="haraw")
-        bb16 = const.tile([P, H3], BF16, name="bb16")
-        nc.scalar.dma_start(out=bb16[:], in_=bEA1.partition_broadcast(P))
+        brow = const.tile([P, P], BF16, name="brow")
+        nc.vector.memset(brow[:].bitcast(I32), 0)
+        nc.scalar.dma_start(out=brow[0:1, :], in_=bEA1.rearrange("(o n) -> o n", o=1))
 
         raws = {}
         hm = const.tile([P, NG, TILES, HD], BF16, name="hm")
-        hm_src = H_mean_M.rearrange("(x q) f -> q x f", q=P)
+        hm_src = H_mean_M.rearrange("(g q i) f -> q g (i f)", q=P, i=TILES)
         wraw = const.tile([P, 4, H3], BF16, name="wraw")
 
         def load_chunk(g0, n):
@@ -75,8 +78,8 @@ def tile_mymodel_icdm_pa_t_kernel(tc, H_A, H_mean_A, H_mean_M, wEA1, bEA1, out):
 
         def load_hm(g0, n):
             nc.sync.dma_start(
-                out=hm[:, g0 : g0 + n, :, :].rearrange("q g i f -> q (g i) f"),
-                in_=hm_src[:, g0 * TILES : (g0 + n) * TILES, :],
+                out=hm[:, g0 : g0 + n, :, :].rearrange("q g i f -> q g (i f)"),
+                in_=hm_src[:, g0 : g0 + n, :],
             )
 
         progress = {"chunk": 0, "group": 0, "part": 0, "hm_group": 0}
@@ -109,7 +112,7 @@ def tile_mymodel_icdm_pa_t_kernel(tc, H_A, H_mean_A, H_mean_M, wEA1, bEA1, out):
         wgrp = const.tile([P, H3, 4], BF16, name="wgrp", align_bytes=64)
         wc = const.tile([P, H3], U32, name="wc", align_bytes=64)
         ws = const.tile([P, H3], U8, name="ws", align_bytes=64)
-        bias = const.tile([P, TILES, H3], F32, name="bias")
+        bias = const.tile([P, 1], F32, name="bias")
 
         def prep_ha_copy():
             nc.vector.tensor_copy(out=hagrp[:], in_=haraw[:].rearrange("p c j h -> p c h j"))
@@ -121,7 +124,9 @@ def tile_mymodel_icdm_pa_t_kernel(tc, H_A, H_mean_A, H_mean_M, wEA1, bEA1, out):
 
         def prep_w():
             nc.vector.tensor_copy(out=wgrp[:], in_=wraw[:].rearrange("p t n -> p n t"))
-            nc.vector.tensor_copy(out=bias[:], in_=bb16[:].unsqueeze(1).to_broadcast([P, TILES, H3]))
+            bcol = ps4p.tile([P, P], BF16, name="bcol", tag="ps4")
+            nc.tensor.transpose(bcol[:], brow[:], ident[:])
+            nc.vector.tensor_copy(out=bias[:], in_=bcol[:, 0:1])
             nc.vector.quantize_mx(
                 out=wc[:].bitcast(FP8X4), scales=ws[:], in_=wgrp[:].rearrange("p n t -> p (n t)")
             )
@@ -135,10 +140,8 @@ def tile_mymodel_icdm_pa_t_kernel(tc, H_A, H_mean_A, H_mean_M, wEA1, bEA1, out):
                 on_scalar = [i0 for i0 in range(0, TILES, 2) if (c, i0) in scalar_units(g)]
                 pieces = [(0, TILES)] if not on_scalar else [(0, 2), (2, 4)]
                 for i0, i1 in pieces:
-                    src = raw[:, c, :, w0 + i0 * P : w0 + i1 * P].rearrange("p t (b a) -> p b t a", a=4)
-                    dst = grp[:, c, i0:i1, :, :].rearrange("p i q t -> p (i q) t").rearrange(
-                        "p (b a) t -> p b t a", a=4
-                    )
+                    src = raw[:, c, :, w0 : w0 + GROUP].rearrange("p t (q i) -> p q t i", i=TILES)[:, :, :, i0:i1]
+                    dst = grp[:, c, i0:i1, :, :].rearrange("p i q t -> p q t i")
                     if i0 in on_scalar:
                         nc.scalar.copy(out=dst, in_=src)
                     else:
@@ -212,37 +215,44 @@ def tile_mymodel_icdm_pa_t_kernel(tc, H_A, H_mean_A, H_mean_M, wEA1, bEA1, out):
 
         def mm2(g):
             codes, plane = st[("c2", g)]
-            ps = ps3p.tile([P, TILES, H3], F32, name="ps3", tag="ps3")
-            for i in range(TILES):
-                cols = slice(i * P, i * P + P)
-                nc.tensor.matmul_mx(
-                    out=ps[:, i, :],
-                    lhsT=codes[:, cols].bitcast(FP8X4),
-                    lhsT_scale=plane[:, cols],
-                    rhs=wc[:].bitcast(FP8X4),
-                    rhs_scale=ws[:],
-                    start=True,
-                    stop=True,
-                )
+            ps = ps3p.tile([P, GROUP], F32, name="ps3", tag="ps3")
+            nc.tensor.matmul_mx(
+                out=ps[:],
+                lhsT=wc[:].bitcast(FP8X4),
+                lhsT_scale=ws[:],
+                rhs=codes[:].bitcast(FP8X4),
+                rhs_scale=plane[:],
+                start=True,
+                stop=True,
+            )
             st[("ps3", g)] = ps
 
-        def add_bias(g):
-            o32 = outp.tile([P, TILES, H3], F32, name="o32", tag="o32")
-            nc.vector.tensor_tensor(out=o32[:], in0=st[("ps3", g)][:], in1=bias[:], op=mybir.AluOpType.add)
-            st[("o32", g)] = o32
+        def bias_relu(g):
+            o_t = outp.tile([P, GROUP], F32, name="o_t", tag="o_t", bufs=3)
+            nc.scalar.activation(
+                out=o_t[:],
+                in_=st[("ps3", g)][:],
+                func=mybir.ActivationFunctionType.Relu,
+                bias=bias[:, 0:1],
+                scale=1.0,
+            )
+            ps = ps4p.tile([P, TILES, H3], F32, name="ps4", tag="ps4")
+            for i in range(TILES):
+                nc.tensor.transpose(ps[:, i, :], o_t[:, i * P : (i + 1) * P], ident32[:])
+            st[("ps4", g)] = ps
 
-        def relu_store(g):
-            o32 = st[("o32", g)]
-            nc.scalar.activation(out=o32[:], in_=o32[:], func=mybir.ActivationFunctionType.Relu)
+        def copy_store(g):
+            o32 = outp.tile([P, TILES, H3], F32, name="o32", tag="o32")
+            nc.scalar.copy(out=o32[:], in_=st[("ps4", g)][:])
             nc.sync.dma_start(
-                out=out[g * GROUP : (g + 1) * GROUP, :].rearrange("(i q) f -> q i f", i=TILES),
-                in_=o32[:],
+                out=out[g * GROUP : (g + 1) * GROUP, :].rearrange("(q i) f -> q (i f)", i=TILES),
+                in_=o32[:].rearrange("p i f -> p (i f)"),
             )
 
         def live(g):
             return 0 <= g < NG
 
-        for s in range(NG + 4):
+        for s in range(NG + 5):
             if live(s):
                 regroup(s)
             if s == 0:
@@ -250,16 +260,16 @@ def tile_mymodel_icdm_pa_t_kernel(tc, H_A, H_mean_A, H_mean_M, wEA1, bEA1, out):
                 prep_ha_quant()
             if s == 1:
                 prep_w()
-            if live(s - 3):
-                add_bias(s - 3)
             if live(s - 2):
                 quant2(s - 2)
                 mm2(s - 2)
             if live(s):
                 quant1(s)
+            if live(s - 4):
+                copy_store(s - 4)
+            if live(s - 3):
+                bias_relu(s - 3)
             if live(s - 1):
                 evac(s - 1)
             if live(s):
                 mm1(s)
-            if live(s - 3):
-                relu_store(s - 3)

@@ -27,7 +27,7 @@ PINNED = False
 
 
 def scalar_units(g):
-    return [(1, 0), (1, 2)] if g < 2 else ([(1, 2)] if g % 3 == 0 else [])
+    return [(1, 0), (1, 2)] if g < 2 else ([(1, 2)] if g < 13 and g % 4 != 1 else [])
 
 
 def vector_evacs(g):

@@ -145,7 +145,10 @@ def tile_mymodel_icdm_pa_t_kernel(tc, H_A, H_mean_A, H_mean_M, wEA1, bEA1, out):
                     if i0 in on_scalar:
                         nc.scalar.copy(out=dst, in_=src)
                     else:
-                        nc.vector.tensor_copy(out=dst, in_=src)
+                        nc.vector.tensor_copy(
+                            out=dst.rearrange("p (r s) t i -> p r t i s", s=2),
+                            in_=src.rearrange("p (r s) t i -> p r t i s", s=2),
+                        )
             st[("grp", g)] = grp
             if g + 1 == NG or raws[g + 1][1] == 0:
                 load_next()

@@ -16,22 +16,26 @@ P = 128
 HD = 256
 H3 = 128
 EVENTS = 8192
-GROUP = 512
-TILES = 4
-NG = EVENTS // GROUP
-CHUNKS = [1,1,1,1,2,2,2,2,2,1,1]
-HM_PARTS = [2,2,2,2,4,4]
+
+BLOCKS = [(512 * b, 4) for b in range(16)]
+NB = len(BLOCKS)
+LOADS = [[0], [1], [2], [3], [4], [5, 6], [7, 8], [9, 10], [11, 12], [13, 14], [15]]
 RAW_BUFS = 3
+HM_LOADS = [[0, 1], [2, 3], [4, 5], [6, 7], [8, 9, 10, 11], [12, 13, 14, 15]]
+UNITS = [(b, 0, BLOCKS[b][1]) for b in range(NB - 1)] + [(NB - 1, 0, 2), (NB - 1, 2, 4)]
+NU = len(UNITS)
 ODD_PLANE = (2, 0, 0)
-PINNED = False
 
 
-def scalar_units(g):
-    return [(1, 0), (1, 2)] if g < 2 else ([(1, 2)] if g < 13 and g % 4 != 1 else [])
+def scalar_pieces(u):
+    if u == 1:
+        return [(1, 0, 2), (1, 2, 4)]
+    return [(1, 2, 4)] if u < 13 and u % 4 != 1 else []
 
 
-def vector_evacs(g):
-    return [2, 3] if g >= NG - 1 else []
+def vector_evacs(u):
+    b, i0, i1 = UNITS[u]
+    return [i1 - 1] if u >= NU - 2 else []
 
 
 def tile_mymodel_icdm_pa_t_kernel(tc, H_A, H_mean_A, H_mean_M, wEA1, bEA1, out):
@@ -44,64 +48,68 @@ def tile_mymodel_icdm_pa_t_kernel(tc, H_A, H_mean_A, H_mean_M, wEA1, bEA1, out):
         ps1p = ctx.enter_context(tc.psum_pool(name="ps1p", bufs=4))
         ps3p = ctx.enter_context(tc.psum_pool(name="ps3p", bufs=2))
         ps4p = ctx.enter_context(tc.psum_pool(name="ps4p", bufs=2))
-        if PINNED:
-            ctx.enter_context(tc.manual_schedule())
 
         ident = const.tile([P, P], BF16, name="ident")
         make_identity(nc, ident[:])
         ident32 = const.tile([P, P], F32, name="ident32")
         make_identity(nc, ident32[:])
         hm32 = const.tile([P, P], F32, name="hm32")
-
         haraw = const.tile([P, 2, 4, HD], BF16, name="haraw")
         brow = const.tile([P, P], BF16, name="brow")
         nc.vector.memset(brow[:].bitcast(I32), 0)
         nc.scalar.dma_start(out=brow[0:1, :], in_=bEA1.rearrange("(o n) -> o n", o=1))
-
-        raws = {}
-        hm = const.tile([P, NG, TILES, HD], BF16, name="hm")
-        hm_src = H_mean_M.rearrange("(g q i) f -> q g (i f)", q=P, i=TILES)
+        hm = const.tile([P, EVENTS // P, HD], BF16, name="hm")
         wraw = const.tile([P, 4, H3], BF16, name="wraw")
 
-        def load_chunk(g0, n):
-            width = n * GROUP
+        raws = {}
+        last_of_load = {blocks[-1]: k for k, blocks in enumerate(LOADS)}
+
+        def load_ha_blocks(blocks):
+            e0 = BLOCKS[blocks[0]][0]
+            width = sum(BLOCKS[b][1] for b in blocks) * P
             raw = rawp.tile([P, 2, 4, width], BF16, name="raw", tag="raw")
             for c in range(2):
                 nc.sync.dma_start(
                     out=raw[:, c, :, :],
-                    in_=H_A[512 * c : 512 * c + 512, g0 * GROUP : g0 * GROUP + width].rearrange(
-                        "(p j) w -> p j w", j=4
-                    ),
+                    in_=H_A[512 * c : 512 * c + 512, e0 : e0 + width].rearrange("(p j) w -> p j w", j=4),
                 )
-            for d in range(n):
-                raws[g0 + d] = (raw, d * GROUP)
+            for b in blocks:
+                raws[b] = (raw, BLOCKS[b][0] - e0)
 
-        def load_hm(g0, n):
+        def load_hm_blocks(blocks):
+            e0, nt = BLOCKS[blocks[0]]
+            if any(BLOCKS[b][1] != nt for b in blocks):
+                raise ValueError("one load of H_mean_M holds blocks of one size")
+            n = len(blocks) * nt
             nc.sync.dma_start(
-                out=hm[:, g0 : g0 + n, :, :].rearrange("q g i f -> q g (i f)"),
-                in_=hm_src[:, g0 : g0 + n, :],
+                out=hm[:, e0 // P : e0 // P + n, :].rearrange("q (b i) f -> q b (i f)", i=nt),
+                in_=H_mean_M[e0 : e0 + n * P, :].rearrange("(b q i) f -> q b (i f)", q=P, i=nt),
             )
 
-        progress = {"chunk": 0, "group": 0, "part": 0, "hm_group": 0}
+        def load_haraw():
+            nc.sync.dma_start(
+                out=haraw[:].rearrange("p c j h -> p c (j h)"),
+                in_=H_mean_A.rearrange("(c p j) h -> p c (j h)", c=2, j=4),
+            )
+
+        def load_w():
+            nc.sync.dma_start(out=wraw[:], in_=wEA1.rearrange("(t p) n -> p t n", p=P))
+
+        progress = {"load": 0, "hm": 0}
 
         def load_next():
-            k = progress["chunk"]
-            if k >= len(CHUNKS):
+            k = progress["load"]
+            if k >= len(LOADS):
                 return
-            load_chunk(progress["group"], CHUNKS[k])
+            load_ha_blocks(LOADS[k])
             if k == 0:
-                nc.sync.dma_start(
-                    out=haraw[:].rearrange("p c j h -> p c (j h)"),
-                    in_=H_mean_A.rearrange("(c p j) h -> p c (j h)", c=2, j=4),
-                )
+                load_haraw()
             if k == 1:
-                nc.sync.dma_start(out=wraw[:], in_=wEA1.rearrange("(t p) n -> p t n", p=P))
-            progress["chunk"] = k + 1
-            progress["group"] += CHUNKS[k]
-            while progress["part"] < len(HM_PARTS) and progress["hm_group"] < progress["group"] - 1:
-                load_hm(progress["hm_group"], HM_PARTS[progress["part"]])
-                progress["hm_group"] += HM_PARTS[progress["part"]]
-                progress["part"] += 1
+                load_w()
+            progress["load"] = k + 1
+            while progress["hm"] < len(HM_LOADS) and HM_LOADS[progress["hm"]][0] <= LOADS[k][-1] - 1:
+                load_hm_blocks(HM_LOADS[progress["hm"]])
+                progress["hm"] += 1
 
         for k in range(RAW_BUFS):
             load_next()
@@ -115,110 +123,121 @@ def tile_mymodel_icdm_pa_t_kernel(tc, H_A, H_mean_A, H_mean_M, wEA1, bEA1, out):
         bias = const.tile([P, 1], F32, name="bias")
 
         def prep_ha_copy():
-            nc.vector.tensor_copy(out=hagrp[:], in_=haraw[:].rearrange("p c j h -> p c h j"))
+            nc.vector.tensor_copy(out=hagrp[:, 0, :, :], in_=haraw[:, 0, :, :].rearrange("p j h -> p h j"))
+            nc.scalar.copy(out=hagrp[:, 1, :, :], in_=haraw[:, 1, :, :].rearrange("p j h -> p h j"))
 
         def prep_ha_quant():
             nc.vector.quantize_mx(
                 out=hac[:].bitcast(FP8X4), scales=has[:], in_=hagrp[:].rearrange("p c h j -> p (c h j)")
             )
 
-        def prep_w():
-            nc.vector.tensor_copy(out=wgrp[:], in_=wraw[:].rearrange("p t n -> p n t"))
+        def prep_bias():
             bcol = ps4p.tile([P, P], BF16, name="bcol", tag="ps4")
             nc.tensor.transpose(bcol[:], brow[:], ident[:])
             nc.vector.tensor_copy(out=bias[:], in_=bcol[:, 0:1])
+
+        def prep_w_copy():
+            nc.vector.tensor_copy(out=wgrp[:], in_=wraw[:].rearrange("p t n -> p n t"))
+
+        def prep_w_quant():
             nc.vector.quantize_mx(
                 out=wc[:].bitcast(FP8X4), scales=ws[:], in_=wgrp[:].rearrange("p n t -> p (n t)")
             )
 
         st = {}
 
-        def regroup(g):
-            raw, w0 = raws[g]
-            grp = work.tile([P, 2, TILES, P, 4], BF16, name="grp", tag="grp", align_bytes=64)
+        def regroup(u):
+            b, i0, i1 = UNITS[u]
+            nt = BLOCKS[b][1]
+            n = i1 - i0
+            raw, w0 = raws[b]
+            grp = work.tile([P, 2, n, P, 4], BF16, name="grp", tag="grp", align_bytes=64)
             for c in range(2):
-                on_scalar = [i0 for i0 in range(0, TILES, 2) if (c, i0) in scalar_units(g)]
-                pieces = [(0, TILES)] if not on_scalar else [(0, 2), (2, 4)]
-                for i0, i1 in pieces:
-                    src = raw[:, c, :, w0 : w0 + GROUP].rearrange("p t (q i) -> p q t i", i=TILES)[:, :, :, i0:i1]
-                    dst = grp[:, c, i0:i1, :, :].rearrange("p i q t -> p q t i")
-                    if i0 in on_scalar:
+                mine = [(x, y) for cc, x, y in scalar_pieces(u) if cc == c]
+                cuts = sorted(set([i0, i1] + [z for xy in mine for z in xy]))
+                for x, y in zip(cuts, cuts[1:]):
+                    src = raw[:, c, :, w0 : w0 + nt * P].rearrange("p t (r e i) -> p r t i e", e=2, i=nt)[:, :, :, x:y]
+                    dst = grp[:, c, x - i0 : y - i0, :, :].rearrange("p i (r e) t -> p r t i e", e=2)
+                    if (x, y) in mine:
                         nc.scalar.copy(out=dst, in_=src)
                     else:
-                        nc.vector.tensor_copy(
-                            out=dst.rearrange("p (r s) t i -> p r t i s", s=2),
-                            in_=src.rearrange("p (r s) t i -> p r t i s", s=2),
-                        )
-            st[("grp", g)] = grp
-            if g + 1 == NG or raws[g + 1][1] == 0:
+                        nc.vector.tensor_copy(out=dst, in_=src)
+            st[("grp", u)] = grp
+            if i1 == nt and b in last_of_load:
                 load_next()
 
-        def quant1(g):
-            grp = st[("grp", g)]
-            codes = work.tile([P, 2 * GROUP], U32, name="codes1", tag="codes1", align_bytes=64)
-            plane = work.tile([P, 2 * GROUP], U8, name="plane1", tag="plane1", align_bytes=64)
+        def quant1(u):
+            b, i0, i1 = UNITS[u]
+            n = i1 - i0
+            grp = st[("grp", u)]
+            codes = work.tile([P, 2, n * P], U32, name="codes1", tag="codes1", align_bytes=64)
+            plane = work.tile([P, 2, n * P], U8, name="plane1", tag="plane1", align_bytes=64)
             nc.vector.quantize_mx(
-                out=codes[:].bitcast(FP8X4),
-                scales=plane[:],
+                out=codes[:].rearrange("p c w -> p (c w)").bitcast(FP8X4),
+                scales=plane[:].rearrange("p c w -> p (c w)"),
                 in_=grp[:].rearrange("p c i q t -> p (c i q t)"),
             )
-            st[("c1", g)] = (codes, plane)
+            st[("c1", u)] = (codes, plane)
 
-        def mm1(g):
-            codes, plane = st[("c1", g)]
-            for i in range(TILES):
+        def mm1(u):
+            b, i0, i1 = UNITS[u]
+            codes, plane = st[("c1", u)]
+            for i in range(i0, i1):
                 ps = ps1p.tile([P, 4, P], F32, name="ps1", tag="ps1")
+                row = BLOCKS[b][0] // P + i
                 for t in range(2):
-                    if (g, i, t) == ODD_PLANE:
-                        nc.gpsimd.tensor_copy(out=hm32[:], in_=hm[:, g, i, P * t : P * t + P])
+                    if (b, i, t) == ODD_PLANE:
+                        nc.gpsimd.tensor_copy(out=hm32[:], in_=hm[:, row, P * t : P * t + P])
                         nc.tensor.transpose(ps[:, t, :], hm32[:], ident32[:])
                     else:
                         nc.tensor.matmul(
-                            out=ps[:, t, :],
-                            lhsT=hm[:, g, i, P * t : P * t + P],
-                            rhs=ident[:],
-                            start=True,
-                            stop=True,
+                            out=ps[:, t, :], lhsT=hm[:, row, P * t : P * t + P], rhs=ident[:], start=True, stop=True
                         )
+                cols = slice((i - i0) * P, (i - i0) * P + P)
                 for e in range(2):
                     for c in range(2):
-                        cols = slice(c * GROUP + i * P, c * GROUP + i * P + P)
                         hcols = slice(c * HD + e * P, c * HD + e * P + P)
                         nc.tensor.matmul_mx(
                             out=ps[:, 2 + e, :],
                             lhsT=hac[:, hcols].bitcast(FP8X4),
                             lhsT_scale=has[:, hcols],
-                            rhs=codes[:, cols].bitcast(FP8X4),
-                            rhs_scale=plane[:, cols],
+                            rhs=codes[:, c, cols].bitcast(FP8X4),
+                            rhs_scale=plane[:, c, cols],
                             start=(c == 0),
                             stop=(c == 1),
                         )
-                st[("ps1", g, i)] = ps
+                st[("ps1", u, i)] = ps
 
-        def evac(g):
-            grp2 = work.tile([P, TILES, P, 4], BF16, name="grp2", tag="grp2", align_bytes=64)
-            for i in range(TILES):
-                ps = st[("ps1", g, i)]
-                if i in vector_evacs(g):
-                    nc.vector.tensor_copy(out=grp2[:, i, :, :], in_=ps[:].rearrange("p t q -> p q t"))
+        def evac(u, tiles):
+            b, i0, i1 = UNITS[u]
+            if ("grp2", u) not in st:
+                st[("grp2", u)] = work.tile([P, i1 - i0, P, 4], BF16, name="grp2", tag="grp2", align_bytes=64)
+            grp2 = st[("grp2", u)]
+            for i in tiles:
+                ps = st[("ps1", u, i)]
+                dst = grp2[:, i - i0, :, :]
+                src = ps[:].rearrange("p t q -> p q t")
+                if i in vector_evacs(u):
+                    nc.vector.tensor_copy(out=dst, in_=src)
                 else:
-                    nc.scalar.copy(out=grp2[:, i, :, :], in_=ps[:].rearrange("p t q -> p q t"))
-            st[("grp2", g)] = grp2
+                    nc.scalar.copy(out=dst, in_=src)
 
-        def quant2(g):
-            grp2 = st[("grp2", g)]
-            codes = work.tile([P, GROUP], U32, name="codes2", tag="codes2", align_bytes=64)
-            plane = work.tile([P, GROUP], U8, name="plane2", tag="plane2", align_bytes=64)
+        def quant2(u):
+            b, i0, i1 = UNITS[u]
+            n = i1 - i0
+            codes = work.tile([P, n * P], U32, name="codes2", tag="codes2", align_bytes=64)
+            plane = work.tile([P, n * P], U8, name="plane2", tag="plane2", align_bytes=64)
             nc.vector.quantize_mx(
                 out=codes[:].bitcast(FP8X4),
                 scales=plane[:],
-                in_=grp2[:].rearrange("p i q t -> p (i q t)"),
+                in_=st[("grp2", u)][:].rearrange("p i q t -> p (i q t)"),
             )
-            st[("c2", g)] = (codes, plane)
+            st[("c2", u)] = (codes, plane)
 
-        def mm2(g):
-            codes, plane = st[("c2", g)]
-            ps = ps3p.tile([P, GROUP], F32, name="ps3", tag="ps3")
+        def mm2(u):
+            b, i0, i1 = UNITS[u]
+            codes, plane = st[("c2", u)]
+            ps = ps3p.tile([P, (i1 - i0) * P], F32, name="ps3", tag="ps3")
             nc.tensor.matmul_mx(
                 out=ps[:],
                 lhsT=wc[:].bitcast(FP8X4),
@@ -228,51 +247,67 @@ def tile_mymodel_icdm_pa_t_kernel(tc, H_A, H_mean_A, H_mean_M, wEA1, bEA1, out):
                 start=True,
                 stop=True,
             )
-            st[("ps3", g)] = ps
+            st[("ps3", u)] = ps
 
-        def bias_relu(g):
-            o_t = outp.tile([P, GROUP], F32, name="o_t", tag="o_t", bufs=3)
+        def bias_relu(u):
+            b, i0, i1 = UNITS[u]
+            o_t = outp.tile([P, (i1 - i0) * P], F32, name="o_t", tag="o_t", bufs=3)
             nc.scalar.activation(
                 out=o_t[:],
-                in_=st[("ps3", g)][:],
+                in_=st[("ps3", u)][:],
                 func=mybir.ActivationFunctionType.Relu,
                 bias=bias[:, 0:1],
                 scale=1.0,
             )
-            ps = ps4p.tile([P, TILES, H3], F32, name="ps4", tag="ps4")
-            for i in range(TILES):
-                nc.tensor.transpose(ps[:, i, :], o_t[:, i * P : (i + 1) * P], ident32[:])
-            st[("ps4", g)] = ps
+            st[("o_t", u)] = o_t
 
-        def copy_store(g):
-            o32 = outp.tile([P, TILES, H3], F32, name="o32", tag="o32")
-            nc.scalar.copy(out=o32[:], in_=st[("ps4", g)][:])
+        def turn(u):
+            b, i0, i1 = UNITS[u]
+            o_t = st[("o_t", u)]
+            ps = ps4p.tile([P, i1 - i0, H3], F32, name="ps4", tag="ps4")
+            for i in range(i1 - i0):
+                nc.tensor.transpose(ps[:, i, :], o_t[:, i * P : (i + 1) * P], ident32[:])
+            st[("ps4", u)] = ps
+
+        def copy_store(u):
+            b, i0, i1 = UNITS[u]
+            e0, nt = BLOCKS[b]
+            o32 = outp.tile([P, i1 - i0, H3], F32, name="o32", tag="o32")
+            if u >= NU - 3:
+                nc.vector.tensor_copy(out=o32[:], in_=st[("ps4", u)][:])
+            else:
+                nc.scalar.copy(out=o32[:], in_=st[("ps4", u)][:])
             nc.sync.dma_start(
-                out=out[g * GROUP : (g + 1) * GROUP, :].rearrange("(q i) f -> q (i f)", i=TILES),
-                in_=o32[:].rearrange("p i f -> p (i f)"),
+                out=out[e0 : e0 + nt * P, :].rearrange("(q i) f -> q i f", i=nt)[:, i0:i1, :],
+                in_=o32[:],
             )
 
-        def live(g):
-            return 0 <= g < NG
+        def live(u):
+            return 0 <= u < NU
 
-        for s in range(NG + 5):
+        prep_bias()
+        for s in range(NU + 5):
             if live(s):
                 regroup(s)
             if s == 0:
                 prep_ha_copy()
-                prep_ha_quant()
             if s == 1:
-                prep_w()
+                prep_w_copy()
             if live(s - 2):
                 quant2(s - 2)
                 mm2(s - 2)
             if live(s):
                 quant1(s)
+            if s == 0:
+                prep_ha_quant()
+            if s == 1:
+                prep_w_quant()
             if live(s - 4):
                 copy_store(s - 4)
             if live(s - 3):
                 bias_relu(s - 3)
+                turn(s - 3)
             if live(s - 1):
-                evac(s - 1)
+                evac(s - 1, range(UNITS[s - 1][1], UNITS[s - 1][2]))
             if live(s):
                 mm1(s)

from contextlib import ExitStack

import concourse.mybir as mybir
from concourse.masks import make_identity

FLOPS = 2 * 1024 * 8192 * 256 + 2 * 8192 * 512 * 128

BF16 = mybir.dt.bfloat16
F32 = mybir.dt.float32
U32 = mybir.dt.uint32
U8 = mybir.dt.uint8
I32 = mybir.dt.int32
FP8X4 = mybir.dt.float8_e4m3fn_x4

P = 128
HD = 256
H3 = 128
EVENTS = 8192

BLOCKS = [(512 * b, 4) for b in range(16)]
NB = len(BLOCKS)
LOADS = [[0], [1], [2], [3], [4], [5, 6], [7, 8], [9, 10], [11, 12], [13, 14], [15]]
RAW_BUFS = 3
HM_LOADS = [[0, 1], [2, 3], [4, 5], [6, 7], [8, 9, 10, 11], [12, 13, 14, 15]]
UNITS = [(b, 0, BLOCKS[b][1]) for b in range(NB - 1)] + [(NB - 1, 0, 2), (NB - 1, 2, 4)]
NU = len(UNITS)
ODD_PLANE = (2, 0, 0)


def scalar_pieces(u):
    if u == 1:
        return [(1, 0, 2), (1, 2, 4)]
    return [(1, 2, 4)] if u < 13 and u % 4 != 1 else []


def vector_evacs(u):
    b, i0, i1 = UNITS[u]
    return [i1 - 1] if u >= NU - 2 else []


def tile_mymodel_icdm_pa_t_kernel(tc, H_A, H_mean_A, H_mean_M, wEA1, bEA1, out):
    nc = tc.nc
    with ExitStack() as ctx:
        const = ctx.enter_context(tc.tile_pool(name="const", bufs=1))
        rawp = ctx.enter_context(tc.tile_pool(name="rawp", bufs=RAW_BUFS))
        work = ctx.enter_context(tc.tile_pool(name="work", bufs=3))
        outp = ctx.enter_context(tc.tile_pool(name="outp", bufs=8))
        ps1p = ctx.enter_context(tc.psum_pool(name="ps1p", bufs=4))
        ps3p = ctx.enter_context(tc.psum_pool(name="ps3p", bufs=2))
        ps4p = ctx.enter_context(tc.psum_pool(name="ps4p", bufs=2))

        ident = const.tile([P, P], BF16, name="ident")
        make_identity(nc, ident[:])
        ident32 = const.tile([P, P], F32, name="ident32")
        make_identity(nc, ident32[:])
        hm32 = const.tile([P, P], F32, name="hm32")
        haraw = const.tile([P, 2, 4, HD], BF16, name="haraw")
        brow = const.tile([P, P], BF16, name="brow")
        nc.vector.memset(brow[:].bitcast(I32), 0)
        nc.scalar.dma_start(out=brow[0:1, :], in_=bEA1.rearrange("(o n) -> o n", o=1))
        hm = const.tile([P, EVENTS // P, HD], BF16, name="hm")
        wraw = const.tile([P, 4, H3], BF16, name="wraw")

        raws = {}
        last_of_load = {blocks[-1]: k for k, blocks in enumerate(LOADS)}

        def load_ha_blocks(blocks):
            e0 = BLOCKS[blocks[0]][0]
            width = sum(BLOCKS[b][1] for b in blocks) * P
            raw = rawp.tile([P, 2, 4, width], BF16, name="raw", tag="raw")
            for c in range(2):
                nc.sync.dma_start(
                    out=raw[:, c, :, :],
                    in_=H_A[512 * c : 512 * c + 512, e0 : e0 + width].rearrange("(p j) w -> p j w", j=4),
                )
            for b in blocks:
                raws[b] = (raw, BLOCKS[b][0] - e0)

        def load_hm_blocks(blocks):
            e0, nt = BLOCKS[blocks[0]]
            if any(BLOCKS[b][1] != nt for b in blocks):
                raise ValueError("one load of H_mean_M holds blocks of one size")
            n = len(blocks) * nt
            nc.sync.dma_start(
                out=hm[:, e0 // P : e0 // P + n, :].rearrange("q (b i) f -> q b (i f)", i=nt),
                in_=H_mean_M[e0 : e0 + n * P, :].rearrange("(b q i) f -> q b (i f)", q=P, i=nt),
            )

        def load_haraw():
            nc.sync.dma_start(
                out=haraw[:].rearrange("p c j h -> p c (j h)"),
                in_=H_mean_A.rearrange("(c p j) h -> p c (j h)", c=2, j=4),
            )

        def load_w():
            nc.sync.dma_start(out=wraw[:], in_=wEA1.rearrange("(t p) n -> p t n", p=P))

        progress = {"load": 0, "hm": 0}

        def load_next():
            k = progress["load"]
            if k >= len(LOADS):
                return
            load_ha_blocks(LOADS[k])
            if k == 0:
                load_haraw()
            if k == 1:
                load_w()
            progress["load"] = k + 1
            while progress["hm"] < len(HM_LOADS) and HM_LOADS[progress["hm"]][0] <= LOADS[k][-1] - 1:
                load_hm_blocks(HM_LOADS[progress["hm"]])
                progress["hm"] += 1

        for k in range(RAW_BUFS):
            load_next()

        hagrp = const.tile([P, 2, HD, 4], BF16, name="hagrp", align_bytes=64)
        hac = const.tile([P, 2 * HD], U32, name="hac", align_bytes=64)
        has = const.tile([P, 2 * HD], U8, name="has", align_bytes=64)
        wgrp = const.tile([P, H3, 4], BF16, name="wgrp", align_bytes=64)
        wc = const.tile([P, H3], U32, name="wc", align_bytes=64)
        ws = const.tile([P, H3], U8, name="ws", align_bytes=64)
        bias = const.tile([P, 1], F32, name="bias")

        def prep_ha_copy():
            nc.vector.tensor_copy(out=hagrp[:, 0, :, :], in_=haraw[:, 0, :, :].rearrange("p j h -> p h j"))
            nc.scalar.copy(out=hagrp[:, 1, :, :], in_=haraw[:, 1, :, :].rearrange("p j h -> p h j"))

        def prep_ha_quant():
            nc.vector.quantize_mx(
                out=hac[:].bitcast(FP8X4), scales=has[:], in_=hagrp[:].rearrange("p c h j -> p (c h j)")
            )

        def prep_bias():
            bcol = ps4p.tile([P, P], BF16, name="bcol", tag="ps4")
            nc.tensor.transpose(bcol[:], brow[:], ident[:])
            nc.vector.tensor_copy(out=bias[:], in_=bcol[:, 0:1])

        def prep_w_copy():
            nc.vector.tensor_copy(out=wgrp[:], in_=wraw[:].rearrange("p t n -> p n t"))

        def prep_w_quant():
            nc.vector.quantize_mx(
                out=wc[:].bitcast(FP8X4), scales=ws[:], in_=wgrp[:].rearrange("p n t -> p (n t)")
            )

        st = {}

        def regroup(u):
            b, i0, i1 = UNITS[u]
            nt = BLOCKS[b][1]
            n = i1 - i0
            raw, w0 = raws[b]
            grp = work.tile([P, 2, n, P, 4], BF16, name="grp", tag="grp", align_bytes=64)
            for c in range(2):
                mine = [(x, y) for cc, x, y in scalar_pieces(u) if cc == c]
                cuts = sorted(set([i0, i1] + [z for xy in mine for z in xy]))
                for x, y in zip(cuts, cuts[1:]):
                    src = raw[:, c, :, w0 : w0 + nt * P].rearrange("p t (r e i) -> p r t i e", e=2, i=nt)[:, :, :, x:y]
                    dst = grp[:, c, x - i0 : y - i0, :, :].rearrange("p i (r e) t -> p r t i e", e=2)
                    if (x, y) in mine:
                        nc.scalar.copy(out=dst, in_=src)
                    else:
                        nc.vector.tensor_copy(out=dst, in_=src)
            st[("grp", u)] = grp
            if i1 == nt and b in last_of_load:
                load_next()

        def quant1(u):
            b, i0, i1 = UNITS[u]
            n = i1 - i0
            grp = st[("grp", u)]
            codes = work.tile([P, 2, n * P], U32, name="codes1", tag="codes1", align_bytes=64)
            plane = work.tile([P, 2, n * P], U8, name="plane1", tag="plane1", align_bytes=64)
            nc.vector.quantize_mx(
                out=codes[:].rearrange("p c w -> p (c w)").bitcast(FP8X4),
                scales=plane[:].rearrange("p c w -> p (c w)"),
                in_=grp[:].rearrange("p c i q t -> p (c i q t)"),
            )
            st[("c1", u)] = (codes, plane)

        def mm1(u):
            b, i0, i1 = UNITS[u]
            codes, plane = st[("c1", u)]
            for i in range(i0, i1):
                ps = ps1p.tile([P, 4, P], F32, name="ps1", tag="ps1")
                row = BLOCKS[b][0] // P + i
                for t in range(2):
                    if (b, i, t) == ODD_PLANE:
                        nc.gpsimd.tensor_copy(out=hm32[:], in_=hm[:, row, P * t : P * t + P])
                        nc.tensor.transpose(ps[:, t, :], hm32[:], ident32[:])
                    else:
                        nc.tensor.matmul(
                            out=ps[:, t, :], lhsT=hm[:, row, P * t : P * t + P], rhs=ident[:], start=True, stop=True
                        )
                cols = slice((i - i0) * P, (i - i0) * P + P)
                for e in range(2):
                    for c in range(2):
                        hcols = slice(c * HD + e * P, c * HD + e * P + P)
                        nc.tensor.matmul_mx(
                            out=ps[:, 2 + e, :],
                            lhsT=hac[:, hcols].bitcast(FP8X4),
                            lhsT_scale=has[:, hcols],
                            rhs=codes[:, c, cols].bitcast(FP8X4),
                            rhs_scale=plane[:, c, cols],
                            start=(c == 0),
                            stop=(c == 1),
                        )
                st[("ps1", u, i)] = ps

        def evac(u, tiles):
            b, i0, i1 = UNITS[u]
            if ("grp2", u) not in st:
                st[("grp2", u)] = work.tile([P, i1 - i0, P, 4], BF16, name="grp2", tag="grp2", align_bytes=64)
            grp2 = st[("grp2", u)]
            for i in tiles:
                ps = st[("ps1", u, i)]
                dst = grp2[:, i - i0, :, :]
                src = ps[:].rearrange("p t q -> p q t")
                if i in vector_evacs(u):
                    nc.vector.tensor_copy(out=dst, in_=src)
                else:
                    nc.scalar.copy(out=dst, in_=src)

        def quant2(u):
            b, i0, i1 = UNITS[u]
            n = i1 - i0
            codes = work.tile([P, n * P], U32, name="codes2", tag="codes2", align_bytes=64)
            plane = work.tile([P, n * P], U8, name="plane2", tag="plane2", align_bytes=64)
            nc.vector.quantize_mx(
                out=codes[:].bitcast(FP8X4),
                scales=plane[:],
                in_=st[("grp2", u)][:].rearrange("p i q t -> p (i q t)"),
            )
            st[("c2", u)] = (codes, plane)

        def mm2(u):
            b, i0, i1 = UNITS[u]
            codes, plane = st[("c2", u)]
            ps = ps3p.tile([P, (i1 - i0) * P], F32, name="ps3", tag="ps3")
            nc.tensor.matmul_mx(
                out=ps[:],
                lhsT=wc[:].bitcast(FP8X4),
                lhsT_scale=ws[:],
                rhs=codes[:].bitcast(FP8X4),
                rhs_scale=plane[:],
                start=True,
                stop=True,
            )
            st[("ps3", u)] = ps

        def bias_relu(u):
            b, i0, i1 = UNITS[u]
            o_t = outp.tile([P, (i1 - i0) * P], F32, name="o_t", tag="o_t", bufs=3)
            nc.scalar.activation(
                out=o_t[:],
                in_=st[("ps3", u)][:],
                func=mybir.ActivationFunctionType.Relu,
                bias=bias[:, 0:1],
                scale=1.0,
            )
            st[("o_t", u)] = o_t

        def turn(u):
            b, i0, i1 = UNITS[u]
            o_t = st[("o_t", u)]
            ps = ps4p.tile([P, i1 - i0, H3], F32, name="ps4", tag="ps4")
            for i in range(i1 - i0):
                nc.tensor.transpose(ps[:, i, :], o_t[:, i * P : (i + 1) * P], ident32[:])
            st[("ps4", u)] = ps

        def copy_store(u):
            b, i0, i1 = UNITS[u]
            e0, nt = BLOCKS[b]
            o32 = outp.tile([P, i1 - i0, H3], F32, name="o32", tag="o32")
            if u >= NU - 3:
                nc.vector.tensor_copy(out=o32[:], in_=st[("ps4", u)][:])
            else:
                nc.scalar.copy(out=o32[:], in_=st[("ps4", u)][:])
            nc.sync.dma_start(
                out=out[e0 : e0 + nt * P, :].rearrange("(q i) f -> q i f", i=nt)[:, i0:i1, :],
                in_=o32[:],
            )

        def live(u):
            return 0 <= u < NU

        prep_bias()
        for s in range(NU + 5):
            if live(s):
                regroup(s)
            if s == 0:
                prep_ha_copy()
            if s == 1:
                prep_w_copy()
            if live(s - 2):
                quant2(s - 2)
                mm2(s - 2)
            if live(s):
                quant1(s)
            if s == 0:
                prep_ha_quant()
            if s == 1:
                prep_w_quant()
            if live(s - 4):
                copy_store(s - 4)
            if live(s - 3):
                bias_relu(s - 3)
                turn(s - 3)
            if live(s - 1):
                evac(s - 1, range(UNITS[s - 1][1], UNITS[s - 1][2]))
            if live(s):
                mm1(s)
